import numpy as np
import ml_dtypes

BF16 = ml_dtypes.bfloat16


def bf(x):
    return np.asarray(x, np.float32).astype(BF16)


def f32(x):
    return np.asarray(x, np.float32)


def f64(x):
    return np.asarray(x).astype(np.float64)


def striped(idx):
    return np.tile(idx.reshape(-1, 16).T, (8, 1))


D, S, E, NC, M, N = 128, 1024, 4, 128, 512, 1024
LENGTH_SCALE = 0.1


def setup_inputs():
    return {"table": bf(np.random.standard_normal((D, S))), "w": bf(0.15 * np.random.standard_normal((D, M)) / np.sqrt(D)), "csum": f32(0.2 * np.random.standard_normal((NC, E))), "cnum": f32(1.0 + np.random.uniform(size=(NC, 1))), "offs": striped(np.random.permutation(np.tile(np.arange(S), 2))[:N])}


def reference(table, w, csum, cnum, offs):
    idx = offs[:16].T.reshape(-1)
    z = (f64(w).T @ f64(table)[:, idx]).reshape(E, NC, N)
    cen = (f64(csum) / f64(cnum)).T[:, :, None]
    sq = np.mean((z - cen) ** 2, axis=0)
    return np.exp(-sq / (2.0 * LENGTH_SCALE ** 2))

@@ -1,0 +1,74 @@
+import concourse.mybir as mybir
+
+BF16, F32, U16 = mybir.dt.bfloat16, mybir.dt.float32, mybir.dt.uint16
+SQUARE = mybir.ActivationFunctionType.Square
+EXP = mybir.ActivationFunctionType.Exp
+MULT = mybir.AluOpType.mult
+
+P = 128
+S = 1024
+E = 4
+N = 1024
+PIECE = 512
+PIECES = N // PIECE
+HALVES = (slice(0, PIECE // 2), slice(PIECE // 2, PIECE))
+LENGTH_SCALE = 0.1
+
+FLOPS = 2 * P * (E * P) * N
+
+
+def tile_duqclassifier_kernel(tc, table, w, csum, cnum, offs, out):
+    nc = tc.nc
+    with (
+        tc.tile_pool(name="held", bufs=1) as held,
+        tc.tile_pool(name="work", bufs=3) as work,
+        tc.psum_pool(name="psum", bufs=E * PIECES) as psum,
+    ):
+        offsets = held.tile([P, N // 16], U16, name="offsets")
+        nc.sync.dma_start(offsets[:], offs)
+        store = held.tile([P, S], BF16, name="store")
+        nc.sync.dma_start(store[:], table)
+        weights = held.tile([P, E * P], BF16, name="weights")
+        nc.scalar.dma_start(weights[:], w)
+        sums = held.tile([P, E], F32, name="sums")
+        nc.scalar.dma_start(sums[:], csum)
+        counts = held.tile([P, 1], F32, name="counts")
+        nc.scalar.dma_start(counts[:], cnum)
+
+        scratch = held.tile([P, 1], F32, name="scratch")
+        nc.vector.memset(scratch[:], 0.0)
+        nc.scalar.activation(scratch[:], scratch[:], EXP)
+
+        inv_counts = held.tile([P, 1], F32, name="inv_counts")
+        nc.vector.reciprocal(inv_counts[:], counts[:])
+        neg_cen = held.tile([P, E], F32, name="neg_cen")
+        nc.vector.tensor_scalar(neg_cen[:], sums[:], inv_counts[:, 0:1], -1.0, MULT, MULT)
+
+        totals = [held.tile([P, PIECE], F32, name=f"total{piece}") for piece in range(PIECES)]
+        for e in range(E):
+            for piece in range(PIECES):
+                picked = store[:].indirect(
+                    offsets[:, piece * (PIECE // 16) : (piece + 1) * (PIECE // 16)]
+                )
+                z = psum.tile([P, PIECE], F32, name="z")
+                nc.tensor.matmul(z[:], weights[:, e * P : (e + 1) * P], picked, start=True, stop=True)
+                if e == 0:
+                    nc.scalar.activation(totals[piece][:], z[:], SQUARE, bias=neg_cen[:, e : e + 1])
+                else:
+                    sq = work.tile([P, PIECE], F32, name="sq")
+                    nc.scalar.activation(sq[:], z[:], SQUARE, bias=neg_cen[:, e : e + 1])
+                    for half in HALVES if e == E - 1 else (slice(0, PIECE),):
+                        nc.vector.tensor_add(
+                            totals[piece][:, half], totals[piece][:, half], sq[:, half]
+                        )
+
+        for piece in range(PIECES):
+            conf = work.tile([P, PIECE], F32, name="conf")
+            for half in HALVES:
+                nc.scalar.activation(
+                    conf[:, half],
+                    totals[piece][:, half],
+                    EXP,
+                    scale=-1.0 / (E * 2.0 * LENGTH_SCALE**2),
+                )
+            nc.sync.dma_start(out[:, piece * PIECE : (piece + 1) * PIECE], conf[:])

@@ -28,12 +28,14 @@ def tile_duqclassifier_kernel(tc, table, w, csum, cnum, offs, out):
         nc.sync.dma_start(offsets[:], offs)
         store = held.tile([P, S], BF16, name="store")
         nc.sync.dma_start(store[:], table)
-        weights = held.tile([P, E * P], BF16, name="weights")
-        nc.scalar.dma_start(weights[:], w)
+        w_cols = E // 2 * P
+        weights = [held.tile([P, w_cols], BF16, name=f"weights{h}") for h in range(2)]
+        nc.scalar.dma_start(weights[0][:], w[:, :w_cols])
         sums = held.tile([P, E], F32, name="sums")
         nc.scalar.dma_start(sums[:], csum)
         counts = held.tile([P, 1], F32, name="counts")
         nc.scalar.dma_start(counts[:], cnum)
+        nc.scalar.dma_start(weights[1][:], w[:, w_cols:])
 
         scratch = held.tile([P, 1], F32, name="scratch")
         nc.vector.memset(scratch[:], 0.0)
@@ -51,7 +53,8 @@ def tile_duqclassifier_kernel(tc, table, w, csum, cnum, offs, out):
                     offsets[:, piece * (PIECE // 16) : (piece + 1) * (PIECE // 16)]
                 )
                 z = psum.tile([P, PIECE], F32, name="z")
-                nc.tensor.matmul(z[:], weights[:, e * P : (e + 1) * P], picked, start=True, stop=True)
+                block = weights[e // 2][:, e % 2 * P : (e % 2 + 1) * P]
+                nc.tensor.matmul(z[:], block, picked, start=True, stop=True)
                 if e == 0:
                     nc.scalar.activation(totals[piece][:], z[:], SQUARE, bias=neg_cen[:, e : e + 1])
                 else:

@@ -35,11 +35,11 @@ def tile_duqclassifier_kernel(tc, table, w, csum, cnum, offs, out):
         nc.scalar.dma_start(sums[:], csum)
         counts = held.tile([P, 1], F32, name="counts")
         nc.scalar.dma_start(counts[:], cnum)
-        nc.scalar.dma_start(weights[1][:], w[:, w_cols:])
 
         scratch = held.tile([P, 1], F32, name="scratch")
         nc.vector.memset(scratch[:], 0.0)
         nc.scalar.activation(scratch[:], scratch[:], EXP)
+        nc.scalar.dma_start(weights[1][:], w[:, w_cols:])
 
         inv_counts = held.tile([P, 1], F32, name="inv_counts")
         nc.vector.reciprocal(inv_counts[:], counts[:])

import concourse.mybir as mybir

BF16, F32, U16 = mybir.dt.bfloat16, mybir.dt.float32, mybir.dt.uint16
SQUARE = mybir.ActivationFunctionType.Square
EXP = mybir.ActivationFunctionType.Exp
MULT = mybir.AluOpType.mult

P = 128
S = 1024
E = 4
N = 1024
PIECE = 512
PIECES = N // PIECE
HALVES = (slice(0, PIECE // 2), slice(PIECE // 2, PIECE))
LENGTH_SCALE = 0.1

FLOPS = 2 * P * (E * P) * N


def tile_duqclassifier_kernel(tc, table, w, csum, cnum, offs, out):
    nc = tc.nc
    with (
        tc.tile_pool(name="held", bufs=1) as held,
        tc.tile_pool(name="work", bufs=3) as work,
        tc.psum_pool(name="psum", bufs=E * PIECES) as psum,
    ):
        offsets = held.tile([P, N // 16], U16, name="offsets")
        nc.sync.dma_start(offsets[:], offs)
        store = held.tile([P, S], BF16, name="store")
        nc.sync.dma_start(store[:], table)
        w_cols = E // 2 * P
        weights = [held.tile([P, w_cols], BF16, name=f"weights{h}") for h in range(2)]
        nc.scalar.dma_start(weights[0][:], w[:, :w_cols])
        sums = held.tile([P, E], F32, name="sums")
        nc.scalar.dma_start(sums[:], csum)
        counts = held.tile([P, 1], F32, name="counts")
        nc.scalar.dma_start(counts[:], cnum)

        scratch = held.tile([P, 1], F32, name="scratch")
        nc.vector.memset(scratch[:], 0.0)
        nc.scalar.activation(scratch[:], scratch[:], EXP)
        nc.scalar.dma_start(weights[1][:], w[:, w_cols:])

        inv_counts = held.tile([P, 1], F32, name="inv_counts")
        nc.vector.reciprocal(inv_counts[:], counts[:])
        neg_cen = held.tile([P, E], F32, name="neg_cen")
        nc.vector.tensor_scalar(neg_cen[:], sums[:], inv_counts[:, 0:1], -1.0, MULT, MULT)

        totals = [held.tile([P, PIECE], F32, name=f"total{piece}") for piece in range(PIECES)]
        for e in range(E):
            for piece in range(PIECES):
                picked = store[:].indirect(
                    offsets[:, piece * (PIECE // 16) : (piece + 1) * (PIECE // 16)]
                )
                z = psum.tile([P, PIECE], F32, name="z")
                block = weights[e // 2][:, e % 2 * P : (e % 2 + 1) * P]
                nc.tensor.matmul(z[:], block, picked, start=True, stop=True)
                if e == 0:
                    nc.scalar.activation(totals[piece][:], z[:], SQUARE, bias=neg_cen[:, e : e + 1])
                else:
                    sq = work.tile([P, PIECE], F32, name="sq")
                    nc.scalar.activation(sq[:], z[:], SQUARE, bias=neg_cen[:, e : e + 1])
                    for half in HALVES if e == E - 1 else (slice(0, PIECE),):
                        nc.vector.tensor_add(
                            totals[piece][:, half], totals[piece][:, half], sq[:, half]
                        )

        for piece in range(PIECES):
            conf = work.tile([P, PIECE], F32, name="conf")
            for half in HALVES:
                nc.scalar.activation(
                    conf[:, half],
                    totals[piece][:, half],
                    EXP,
                    scale=-1.0 / (E * 2.0 * LENGTH_SCALE**2),
                )
            nc.sync.dma_start(out[:, piece * PIECE : (piece + 1) * PIECE], conf[:])
